import numpy as np
import ml_dtypes


def mxq(x, axis, fmt="e4m3"):
    dtype, down = {"e4m3": (ml_dtypes.float8_e4m3fn, 7), "e5m2": (ml_dtypes.float8_e5m2, 14)}[fmt]
    v = np.moveaxis(np.asarray(x, np.float32).astype(ml_dtypes.bfloat16).astype(np.float64), axis, -1)
    blocks = v.reshape(v.shape[:-1] + (-1, 32))
    amax = np.abs(blocks).max(-1, keepdims=True)
    byte = np.maximum(np.where(amax > 0, np.frexp(amax)[1] - 1 + 127, 0) - down, 1)
    scale = np.exp2(byte - 127.0)
    codes = (blocks / scale).astype(np.float32).astype(dtype).astype(np.float64)
    return np.moveaxis((codes * scale).reshape(v.shape), -1, axis)


WIDE = False


def mx_kscale(k):
    if not WIDE:
        return np.ones(k)
    levels = np.array([10, -10, 5, -5, 0])
    a = np.random.permutation(np.resize(levels, k // 512 * 4)).reshape(k // 512, 4)
    idx = np.arange(k)
    return np.exp2(a[idx // 512, idx % 128 // 32])


BF16 = ml_dtypes.bfloat16


def bf(x):
    return np.asarray(x, np.float32).astype(BF16)


def f64(x):
    return np.asarray(x).astype(np.float64)


E2M1 = np.array([0.0, 0.5, 1.0, 1.5, 2.0, 3.0, 4.0, 6.0, -0.0, -0.5, -1.0, -1.5, -2.0, -3.0, -4.0, -6.0])


def pack_weight(w, fmt):
    k, n = w.shape
    w = f64(bf(w)).reshape(k // 32, 32, n)
    amax = np.abs(w).max(1)
    if fmt == "e4m3":
        byte = np.frexp(amax)[1] - 1 + 127 - 7
    else:
        mant, ex = np.frexp(amax / 6.0)
        byte = np.where(mant > 0.5, ex, ex - 1) + 127
    byte = np.clip(np.where(amax > 0, byte, 1), 1, 254)
    scaled = (w * np.exp2(127.0 - byte)[:, None, :]).reshape(k, n).astype(np.float32)
    by_word = np.ascontiguousarray(scaled.reshape(k // 512, 128, 4, n).transpose(0, 1, 3, 2))
    if fmt == "e4m3":
        words = by_word.astype(ml_dtypes.float8_e4m3fn).view(np.uint8)
    else:
        c = by_word.astype(ml_dtypes.float4_e2m1fn).view(np.uint8) & 0xF
        words = c[..., 0::2] | (c[..., 1::2] << 4)
    return np.ascontiguousarray(words), np.ascontiguousarray(byte.astype(np.uint8).reshape(k // 512, 16, n))


def unpack_weight(words, scales, fmt):
    g, p, n, _ = words.shape
    if fmt == "e4m3":
        vals = np.ascontiguousarray(words).view(ml_dtypes.float8_e4m3fn).astype(np.float64)
    else:
        nib = np.empty((g, p, n, 4), np.uint8)
        nib[..., 0::2] = words & 0xF
        nib[..., 1::2] = words >> 4
        vals = E2M1[nib]
    vals = vals * np.repeat(np.exp2(scales.astype(np.float64) - 127.0), 8, axis=1)[..., None]
    return vals.transpose(0, 1, 3, 2).reshape(g * 512, n)


B, S, D, O, BS = 1, 128, 4096, 4096, 1024
MULT = D // BS


def fwht(x):
    n = x.shape[-1]
    steps = int(round(np.log2(n)))
    shape = x.shape
    x = x.reshape(-1, n)
    h = 1
    for _ in range(steps):
        x = x.reshape(-1, n // (2 * h), 2, h)
        a = x[:, :, 0, :]
        b = x[:, :, 1, :]
        x = np.stack([a + b, a - b], axis=2).reshape(-1, n)
        h *= 2
    return x.reshape(shape)


def pad_to_block_last(x, blocksize):
    size = x.shape[-1]
    target = ((size - 1) // blocksize + 1) * blocksize
    delta = target - size
    if delta == 0:
        return x
    pad = [(0, 0)] * (x.ndim - 1) + [(0, delta)]
    return np.pad(x, pad)


def block_factors():
    lv = np.unique(mx_kscale(D))
    lv = lv[np.argsort(-np.abs(np.log2(lv)), kind="stable")]
    return np.repeat(lv[np.arange(MULT) % len(lv)], BS)


def setup_inputs():
    s = block_factors()
    input = bf(np.random.standard_normal((B, S, D)) * s)
    weight = np.random.standard_normal((O, D)) / np.sqrt(D) / s[None, :]
    words, scales = pack_weight(np.ascontiguousarray(weight.T), "e4m3")
    return {"input": input, "weight_words": words, "weight_scales": scales}


def reference(input, weight_words, weight_scales):
    x = pad_to_block_last(f64(input), BS)
    lead = x.shape[:-1]
    d = x.shape[-1]
    mult = d // BS
    x = x.reshape(lead + (mult, BS))
    x = fwht(x) * (1.0 / np.sqrt(BS))
    x = x.reshape(lead + (d,))
    return mxq(x, 2, "e4m3") @ unpack_weight(weight_words, weight_scales, "e4m3")

@@ -1,0 +1,149 @@
+from contextlib import ExitStack
+
+import concourse.mybir as mybir
+from concourse.masks import make_identity
+
+BF16 = mybir.dt.bfloat16
+F32 = mybir.dt.float32
+I32 = mybir.dt.int32
+U8 = mybir.dt.uint8
+U32 = mybir.dt.uint32
+FP8X4 = mybir.dt.float8_e4m3fn_x4
+ALU = mybir.AluOpType
+
+P = 128
+D = 4096
+O = 4096
+GROUPS = 8
+NT = 512
+BANKS = 8
+INV = 1.0 / 32.0
+
+FLOPS = 2 * 128 * 4096 * 4096 + 128 * 4096 * 10
+
+
+def tile_hadlinear_w_kernel(tc, x_in, weight_words, weight_scales, out):
+    nc = tc.nc
+    xf = x_in.flatten_outer_dims()
+    of = out.flatten_outer_dims()
+    with ExitStack() as ctx:
+        keep = ctx.enter_context(tc.tile_pool(name="keep", bufs=1))
+        psum = ctx.enter_context(tc.psum_pool(name="psum", bufs=1))
+
+        planes = keep.tile([P, 2, O], U8, name="planes", align_bytes=64)
+        nc.vector.memset(planes[:].bitcast(I32), 0)
+        x_sb = keep.tile([P, D], BF16, name="x_sb", align_bytes=64)
+        for half in range(2):
+            cols = slice(2048 * half, 2048 * (half + 1))
+            nc.sync.dma_start(out=x_sb[:, cols], in_=xf[:, cols])
+        for h in range(2):
+            for q in range(4):
+                nc.sync.dma_start(
+                    out=planes[32 * q : 32 * q + 16, h, :].bitcast(I32),
+                    in_=weight_scales[4 * h : 4 * h + 4, 4 * q : 4 * q + 4, :].bitcast(I32),
+                )
+        w_parts = []
+        for g in range(GROUPS):
+            words = weight_words[g].rearrange("p n t -> p (n t)").bitcast(I32)
+            pieces = 1 if g < GROUPS - 1 else 4
+            width = O // pieces
+            for c in range(pieces):
+                wt = keep.tile([P, width], U32, name="w%d_%d" % (g, c), align_bytes=64)
+                nc.sync.dma_start(out=wt[:].bitcast(I32), in_=words[:, c * width : (c + 1) * width])
+                w_parts.append((g, c * width, wt))
+
+        ident = keep.tile([P, P], F32, name="ident")
+        make_identity(nc, ident[:])
+        ii = keep.tile([P, P], I32, name="ii")
+        jj = keep.tile([P, P], I32, name="jj")
+        nc.gpsimd.iota(ii[:], pattern=[[0, P]], base=0, channel_multiplier=1)
+        nc.gpsimd.iota(jj[:], pattern=[[1, P]], base=0, channel_multiplier=0)
+        par = keep.tile([P, P], I32, name="par")
+        sh = keep.tile([P, P], I32, name="sh")
+        nc.vector.tensor_tensor(out=par[:], in0=ii[:], in1=jj[:], op=ALU.bitwise_and)
+        for s in (4, 2, 1):
+            nc.vector.tensor_single_scalar(out=sh[:], in_=par[:], scalar=s, op=ALU.logical_shift_right)
+            nc.vector.tensor_tensor(out=par[:], in0=par[:], in1=sh[:], op=ALU.bitwise_xor)
+        nc.vector.tensor_single_scalar(out=par[:], in_=par[:], scalar=1, op=ALU.bitwise_and)
+        h_pos = keep.tile([P, P], BF16, name="h_pos")
+        h_neg = keep.tile([P, P], BF16, name="h_neg")
+        nc.vector.tensor_scalar(out=h_pos[:], in0=par[:], scalar1=-2.0, scalar2=1.0, op0=ALU.mult, op1=ALU.add)
+        nc.vector.tensor_scalar(out=h_neg[:], in0=par[:], scalar1=2.0, scalar2=-1.0, op0=ALU.mult, op1=ALU.add)
+
+        xw = x_sb[:].bitcast(F32)
+        xt = keep.tile([P, D], BF16, name="xt")
+        for b in range(4):
+            tb = psum.tile([P, 4, P], F32, name="tb%d" % b, tag="bank%d" % b)
+            for a in range(4):
+                g, u = 2 * b + a // 2, a % 2
+                nc.tensor.transpose(tb[:, a, :], xw[:, 256 * g + u : 256 * (g + 1) : 2], ident[:])
+            dst = xt[:, 1024 * b : 1024 * (b + 1)].bitcast(F32)
+            src = tb[:].rearrange("p a s -> p (a s)")
+            if b % 2 == 0:
+                nc.vector.tensor_copy(out=dst, in_=src)
+            else:
+                nc.scalar.copy(out=dst, in_=src)
+
+        y_codes = keep.tile([P, GROUPS * P], U32, name="y_codes", align_bytes=64)
+        y_planes = keep.tile([P, GROUPS * P], U8, name="y_planes", align_bytes=64)
+        z_banks = [(4, 5), (6, 7), (0, 1), (2, 3)]
+        for b in range(4):
+            stage_a = keep.tile([P, 2, 2, 256], F32, name="stage_a%d" % b)
+            for gp in range(2):
+                zb = psum.tile([P, NT], F32, name="z%d_%d" % (b, gp), tag="bank%d" % z_banks[b][gp])
+                nc.tensor.matmul(zb[:], lhsT=h_pos[:], rhs=xt[:, 1024 * b : 1024 * b + 512], start=True, stop=False)
+                nc.tensor.matmul(
+                    zb[:],
+                    lhsT=(h_pos if gp == 0 else h_neg)[:],
+                    rhs=xt[:, 1024 * b + 512 : 1024 * (b + 1)],
+                    start=False,
+                    stop=True,
+                )
+                pairs = zb[:].rearrange("p (m e) -> p m e", e=2)
+                odd = keep.tile([P, 256], F32, name="odd%d_%d" % (b, gp))
+                nc.scalar.mul(out=odd[:], in_=pairs[:, :, 1], mul=INV)
+                nc.vector.scalar_tensor_tensor(
+                    out=stage_a[:, gp, 0, :], in0=pairs[:, :, 0], scalar=INV, in1=odd[:], op0=ALU.mult, op1=ALU.add
+                )
+                nc.vector.scalar_tensor_tensor(
+                    out=stage_a[:, gp, 1, :], in0=pairs[:, :, 0], scalar=INV, in1=odd[:], op0=ALU.mult, op1=ALU.subtract
+                )
+            yb = keep.tile([P, 2, 4, P], BF16, name="yb%d" % b)
+            nc.vector.tensor_tensor(
+                out=yb[:, :, 0:2, :], in0=stage_a[:, :, :, 0:P], in1=stage_a[:, :, :, P : 2 * P], op=ALU.add
+            )
+            nc.vector.tensor_tensor(
+                out=yb[:, :, 2:4, :], in0=stage_a[:, :, :, 0:P], in1=stage_a[:, :, :, P : 2 * P], op=ALU.subtract
+            )
+            grouped = keep.tile([P, 2, P, 4], BF16, name="grouped%d" % b, align_bytes=64)
+            nc.scalar.copy(out=grouped[:], in_=yb[:].rearrange("p g t s -> p g s t"))
+            nc.vector.quantize_mx(
+                out=y_codes[:, 256 * b : 256 * (b + 1)].bitcast(FP8X4),
+                scales=y_planes[:, 256 * b : 256 * (b + 1)],
+                in_=grouped[:].rearrange("p g s t -> p (g s t)"),
+            )
+
+        acc = []
+        for j in range(BANKS):
+            acc.append(psum.tile([P, NT], F32, name="acc%d" % j, tag="bank%d" % ((j + 4) % BANKS)))
+        for g, first, wt in w_parts:
+            k = 4 * (g % 4)
+            h = g // 4
+            for c in range(wt.shape[1] // NT):
+                j = first // NT + c
+                nc.tensor.matmul_mx(
+                    out=acc[j][:],
+                    lhsT=y_codes[:, P * g : P * (g + 1)].bitcast(FP8X4),
+                    lhsT_scale=y_planes[:, P * g : P * (g + 1)],
+                    rhs=wt[:, NT * c : NT * (c + 1)].bitcast(FP8X4),
+                    rhs_scale=planes[k:P, h, NT * j : NT * (j + 1)],
+                    start=(g == 0),
+                    stop=(g == GROUPS - 1),
+                )
+        for j in range(BANKS):
+            res = keep.tile([P, NT], F32, name="res%d" % j)
+            if j % 2 == 0:
+                nc.vector.tensor_copy(out=res[:], in_=acc[j][:])
+            else:
+                nc.scalar.copy(out=res[:], in_=acc[j][:])
+            nc.sync.dma_start(out=of[:, NT * j : NT * (j + 1)], in_=res[:])

@@ -36,12 +36,6 @@ def tile_hadlinear_w_kernel(tc, x_in, weight_words, weight_scales, out):
         for half in range(2):
             cols = slice(2048 * half, 2048 * (half + 1))
             nc.sync.dma_start(out=x_sb[:, cols], in_=xf[:, cols])
-        for h in range(2):
-            for q in range(4):
-                nc.sync.dma_start(
-                    out=planes[32 * q : 32 * q + 16, h, :].bitcast(I32),
-                    in_=weight_scales[4 * h : 4 * h + 4, 4 * q : 4 * q + 4, :].bitcast(I32),
-                )
         w_parts = []
         for g in range(GROUPS):
             words = weight_words[g].rearrange("p n t -> p (n t)").bitcast(I32)
@@ -58,6 +52,12 @@ def tile_hadlinear_w_kernel(tc, x_in, weight_words, weight_scales, out):
         jj = keep.tile([P, P], I32, name="jj")
         nc.gpsimd.iota(ii[:], pattern=[[0, P]], base=0, channel_multiplier=1)
         nc.gpsimd.iota(jj[:], pattern=[[1, P]], base=0, channel_multiplier=0)
+        for h in range(2):
+            for q in range(4):
+                nc.gpsimd.dma_start(
+                    out=planes[32 * q : 32 * q + 16, h, :].bitcast(F32),
+                    in_=weight_scales[4 * h : 4 * h + 4, 4 * q : 4 * q + 4, :].bitcast(F32),
+                )
         par = keep.tile([P, P], I32, name="par")
         sh = keep.tile([P, P], I32, name="sh")
         nc.vector.tensor_tensor(out=par[:], in0=ii[:], in1=jj[:], op=ALU.bitwise_and)
@@ -126,11 +126,18 @@ def tile_hadlinear_w_kernel(tc, x_in, weight_words, weight_scales, out):
         acc = []
         for j in range(BANKS):
             acc.append(psum.tile([P, NT], F32, name="acc%d" % j, tag="bank%d" % ((j + 4) % BANKS)))
-        for g, first, wt in w_parts:
+        passes = []
+        for pair, groups in ((0, (0, 1)), (1, (0, 1)), (0, (2,)), (1, (2,)), (2, (0, 1, 2)), (3, (0, 1, 2))):
+            for g in groups:
+                for j in (2 * pair, 2 * pair + 1):
+                    passes.append((g, j, w_parts[g][2], j))
+        for g, first, wt in w_parts[3:]:
+            for c in range(wt.shape[1] // NT):
+                passes.append((g, first // NT + c, wt, c))
+        for g, j, wt, c in passes:
             k = 4 * (g % 4)
             h = g // 4
-            for c in range(wt.shape[1] // NT):
-                j = first // NT + c
+            if True:
                 nc.tensor.matmul_mx(
                     out=acc[j][:],
                     lhsT=y_codes[:, P * g : P * (g + 1)].bitcast(FP8X4),

@@ -88,35 +88,63 @@ def tile_hadlinear_w_kernel(tc, x_in, weight_words, weight_scales, out):
         y_planes = keep.tile([P, GROUPS * P], U8, name="y_planes", align_bytes=64)
         z_banks = [(4, 5), (6, 7), (0, 1), (2, 3)]
         for b in range(4):
-            stage_a = keep.tile([P, 2, 2, 256], F32, name="stage_a%d" % b)
+            grouped = keep.tile([P, 2, P, 4], BF16, name="grouped%d" % b, align_bytes=64)
             for gp in range(2):
                 zb = psum.tile([P, NT], F32, name="z%d_%d" % (b, gp), tag="bank%d" % z_banks[b][gp])
-                nc.tensor.matmul(zb[:], lhsT=h_pos[:], rhs=xt[:, 1024 * b : 1024 * b + 512], start=True, stop=False)
-                nc.tensor.matmul(
-                    zb[:],
-                    lhsT=(h_pos if gp == 0 else h_neg)[:],
-                    rhs=xt[:, 1024 * b + 512 : 1024 * (b + 1)],
-                    start=False,
-                    stop=True,
-                )
-                pairs = zb[:].rearrange("p (m e) -> p m e", e=2)
-                odd = keep.tile([P, 256], F32, name="odd%d_%d" % (b, gp))
-                nc.scalar.mul(out=odd[:], in_=pairs[:, :, 1], mul=INV)
-                nc.vector.scalar_tensor_tensor(
-                    out=stage_a[:, gp, 0, :], in0=pairs[:, :, 0], scalar=INV, in1=odd[:], op0=ALU.mult, op1=ALU.add
-                )
-                nc.vector.scalar_tensor_tensor(
-                    out=stage_a[:, gp, 1, :], in0=pairs[:, :, 0], scalar=INV, in1=odd[:], op0=ALU.mult, op1=ALU.subtract
-                )
-            yb = keep.tile([P, 2, 4, P], BF16, name="yb%d" % b)
-            nc.vector.tensor_tensor(
-                out=yb[:, :, 0:2, :], in0=stage_a[:, :, :, 0:P], in1=stage_a[:, :, :, P : 2 * P], op=ALU.add
-            )
-            nc.vector.tensor_tensor(
-                out=yb[:, :, 2:4, :], in0=stage_a[:, :, :, 0:P], in1=stage_a[:, :, :, P : 2 * P], op=ALU.subtract
-            )
-            grouped = keep.tile([P, 2, P, 4], BF16, name="grouped%d" % b, align_bytes=64)
-            nc.scalar.copy(out=grouped[:], in_=yb[:].rearrange("p g t s -> p g s t"))
+                y_view = grouped[:, gp].rearrange("p s (u e) -> p s u e", e=2)
+                if b < 2:
+                    for gl in range(2):
+                        nc.tensor.matmul(
+                            zb[:],
+                            lhsT=(h_neg if gl * gp else h_pos)[:],
+                            rhs=xt[:, 1024 * b + 512 * gl : 1024 * b + 512 * (gl + 1)],
+                            start=(gl == 0),
+                            stop=(gl == 1),
+                        )
+                    pairs = zb[:].rearrange("p (m e) -> p m e", e=2)
+                    odd = keep.tile([P, 2 * P], F32, name="odd%d_%d" % (b, gp))
+                    nc.scalar.mul(out=odd[:], in_=pairs[:, :, 1], mul=INV)
+                    sums = keep.tile([P, 2, 3, P], F32, name="sums%d_%d" % (b, gp))
+                    for e in range(2):
+                        nc.vector.scalar_tensor_tensor(
+                            out=sums[:, e, 0:2, :].rearrange("p u s -> p (u s)"),
+                            in0=pairs[:, :, 0],
+                            scalar=INV,
+                            in1=odd[:],
+                            op0=ALU.mult,
+                            op1=(ALU.subtract if e else ALU.add),
+                        )
+                    nc.scalar.mul(out=sums[:, :, 2, :], in_=sums[:, :, 1, :], mul=-1.0)
+                    nc.vector.tensor_tensor(
+                        out=y_view,
+                        in0=sums[:, :, 0, :].rearrange("p e s -> p s e").unsqueeze(2).to_broadcast([P, P, 2, 2]),
+                        in1=sums[:, :, 1:3, :].rearrange("p e u s -> p s u e"),
+                        op=ALU.add,
+                    )
+                else:
+                    z_view = zb[:].rearrange("p (s u e) -> p s u e", u=2, e=2)
+                    for up in range(2):
+                        for a in range(4):
+                            gl, u = a // 2, a % 2
+                            nc.tensor.matmul(
+                                z_view[:, :, up, :],
+                                lhsT=(h_neg if (gl * gp + u * up) % 2 else h_pos)[:],
+                                rhs=xt[:, 1024 * b + 256 * a : 1024 * b + 256 * (a + 1)].rearrange("p (s e) -> p s e", e=2),
+                                start=(a == 0),
+                                stop=(a == 3),
+                            )
+                    pairs = zb[:].rearrange("p (m e) -> p m e", e=2)
+                    odd = keep.tile([P, 2, 2 * P], F32, name="odd%d_%d" % (b, gp))
+                    for e in range(2):
+                        nc.scalar.mul(out=odd[:, e], in_=pairs[:, :, 1], mul=(-INV if e else INV))
+                    nc.vector.scalar_tensor_tensor(
+                        out=grouped[:, gp].rearrange("p s (u e) -> p (s u) e", e=2),
+                        in0=pairs[:, :, 0].unsqueeze(2).to_broadcast([P, 2 * P, 2]),
+                        scalar=INV,
+                        in1=odd[:].rearrange("p e m -> p m e"),
+                        op0=ALU.mult,
+                        op1=ALU.add,
+                    )
             nc.vector.quantize_mx(
                 out=y_codes[:, 256 * b : 256 * (b + 1)].bitcast(FP8X4),
                 scales=y_planes[:, 256 * b : 256 * (b + 1)],

@@ -18,6 +18,7 @@ GROUPS = 8
 NT = 512
 BANKS = 8
 INV = 1.0 / 32.0
+MAIN = O - NT
 
 FLOPS = 2 * 128 * 4096 * 4096 + 128 * 4096 * 10
 
@@ -36,15 +37,23 @@ def tile_hadlinear_w_kernel(tc, x_in, weight_words, weight_scales, out):
         for half in range(2):
             cols = slice(2048 * half, 2048 * (half + 1))
             nc.sync.dma_start(out=x_sb[:, cols], in_=xf[:, cols])
-        w_parts = []
+        words = weight_words.rearrange("g p n t -> p g (n t)").bitcast(I32)
+        w_main = []
         for g in range(GROUPS):
-            words = weight_words[g].rearrange("p n t -> p (n t)").bitcast(I32)
-            pieces = 1 if g < GROUPS - 1 else 4
-            width = O // pieces
-            for c in range(pieces):
-                wt = keep.tile([P, width], U32, name="w%d_%d" % (g, c), align_bytes=64)
-                nc.sync.dma_start(out=wt[:].bitcast(I32), in_=words[:, c * width : (c + 1) * width])
-                w_parts.append((g, c * width, wt))
+            cuts = [0, MAIN] if g < GROUPS - 1 else [0, MAIN // 2 // NT * NT, MAIN]
+            where = {}
+            for lo, hi in zip(cuts[:-1], cuts[1:]):
+                wt = keep.tile([P, hi - lo], U32, name="w%d_%d" % (g, lo), align_bytes=64)
+                nc.sync.dma_start(out=wt[:].bitcast(I32), in_=words[:, g, lo:hi])
+                for j in range(lo // NT, hi // NT):
+                    where[j] = (wt, NT * j - lo)
+            w_main.append(where)
+        for lo, hi in ((0, 4), (4, 7), (7, 8)):
+            wt = keep.tile([P, hi - lo, NT], U32, name="w_last%d" % lo, align_bytes=64)
+            nc.sync.dma_start(out=wt[:].bitcast(I32), in_=words[:, lo:hi, MAIN:O])
+            flat = wt[:].rearrange("p g n -> p (g n)")
+            for g in range(lo, hi):
+                w_main[g][BANKS - 1] = (flat, NT * (g - lo))
 
         ident = keep.tile([P, P], F32, name="ident")
         make_identity(nc, ident[:])
@@ -155,30 +164,29 @@ def tile_hadlinear_w_kernel(tc, x_in, weight_words, weight_scales, out):
         for j in range(BANKS):
             acc.append(psum.tile([P, NT], F32, name="acc%d" % j, tag="bank%d" % ((j + 4) % BANKS)))
         passes = []
-        for pair, groups in ((0, (0, 1)), (1, (0, 1)), (0, (2,)), (1, (2,)), (2, (0, 1, 2)), (3, (0, 1, 2))):
-            for g in groups:
-                for j in (2 * pair, 2 * pair + 1):
-                    passes.append((g, j, w_parts[g][2], j))
-        for g, first, wt in w_parts[3:]:
-            for c in range(wt.shape[1] // NT):
-                passes.append((g, first // NT + c, wt, c))
-        for g, j, wt, c in passes:
+        for banks in ((0, 1, 2, 3), (4, 5, 6)):
+            passes += [(g, j) for g in range(2) for j in banks]
+        passes += [(g, j) for g in range(2, GROUPS) for j in range(BANKS - 1)]
+        passes += [(g, BANKS - 1) for g in range(GROUPS)]
+        for g, j in passes:
             k = 4 * (g % 4)
             h = g // 4
-            if True:
-                nc.tensor.matmul_mx(
-                    out=acc[j][:],
-                    lhsT=y_codes[:, P * g : P * (g + 1)].bitcast(FP8X4),
-                    lhsT_scale=y_planes[:, P * g : P * (g + 1)],
-                    rhs=wt[:, NT * c : NT * (c + 1)].bitcast(FP8X4),
-                    rhs_scale=planes[k:P, h, NT * j : NT * (j + 1)],
-                    start=(g == 0),
-                    stop=(g == GROUPS - 1),
-                )
-        for j in range(BANKS):
-            res = keep.tile([P, NT], F32, name="res%d" % j)
-            if j % 2 == 0:
-                nc.vector.tensor_copy(out=res[:], in_=acc[j][:])
-            else:
-                nc.scalar.copy(out=res[:], in_=acc[j][:])
-            nc.sync.dma_start(out=of[:, NT * j : NT * (j + 1)], in_=res[:])
+            wt, c = w_main[g][j]
+            nc.tensor.matmul_mx(
+                out=acc[j][:],
+                lhsT=y_codes[:, P * g : P * (g + 1)].bitcast(FP8X4),
+                lhsT_scale=y_planes[:, P * g : P * (g + 1)],
+                rhs=wt[:, c : c + NT].bitcast(FP8X4),
+                rhs_scale=planes[k:P, h, NT * j : NT * (j + 1)],
+                start=(g == 0),
+                stop=(g == GROUPS - 1),
+            )
+        for first, last in ((0, 1), (2, 3), (4, 5), (6, 6), (7, 7)):
+            res = keep.tile([P, NT * (last - first + 1)], F32, name="res%d" % first)
+            for j in range(first, last + 1):
+                dst = res[:, NT * (j - first) : NT * (j - first + 1)]
+                if j % 2 == 0:
+                    nc.vector.tensor_copy(out=dst, in_=acc[j][:])
+                else:
+                    nc.scalar.copy(out=dst, in_=acc[j][:])
+            nc.sync.dma_start(out=of[:, NT * first : NT * (last + 1)], in_=res[:])

@@ -97,63 +97,35 @@ def tile_hadlinear_w_kernel(tc, x_in, weight_words, weight_scales, out):
         y_planes = keep.tile([P, GROUPS * P], U8, name="y_planes", align_bytes=64)
         z_banks = [(4, 5), (6, 7), (0, 1), (2, 3)]
         for b in range(4):
-            grouped = keep.tile([P, 2, P, 4], BF16, name="grouped%d" % b, align_bytes=64)
+            stage_a = keep.tile([P, 2, 2, 256], F32, name="stage_a%d" % b)
             for gp in range(2):
                 zb = psum.tile([P, NT], F32, name="z%d_%d" % (b, gp), tag="bank%d" % z_banks[b][gp])
-                y_view = grouped[:, gp].rearrange("p s (u e) -> p s u e", e=2)
-                if b < 2:
-                    for gl in range(2):
-                        nc.tensor.matmul(
-                            zb[:],
-                            lhsT=(h_neg if gl * gp else h_pos)[:],
-                            rhs=xt[:, 1024 * b + 512 * gl : 1024 * b + 512 * (gl + 1)],
-                            start=(gl == 0),
-                            stop=(gl == 1),
-                        )
-                    pairs = zb[:].rearrange("p (m e) -> p m e", e=2)
-                    odd = keep.tile([P, 2 * P], F32, name="odd%d_%d" % (b, gp))
-                    nc.scalar.mul(out=odd[:], in_=pairs[:, :, 1], mul=INV)
-                    sums = keep.tile([P, 2, 3, P], F32, name="sums%d_%d" % (b, gp))
-                    for e in range(2):
-                        nc.vector.scalar_tensor_tensor(
-                            out=sums[:, e, 0:2, :].rearrange("p u s -> p (u s)"),
-                            in0=pairs[:, :, 0],
-                            scalar=INV,
-                            in1=odd[:],
-                            op0=ALU.mult,
-                            op1=(ALU.subtract if e else ALU.add),
-                        )
-                    nc.scalar.mul(out=sums[:, :, 2, :], in_=sums[:, :, 1, :], mul=-1.0)
-                    nc.vector.tensor_tensor(
-                        out=y_view,
-                        in0=sums[:, :, 0, :].rearrange("p e s -> p s e").unsqueeze(2).to_broadcast([P, P, 2, 2]),
-                        in1=sums[:, :, 1:3, :].rearrange("p e u s -> p s u e"),
-                        op=ALU.add,
-                    )
-                else:
-                    z_view = zb[:].rearrange("p (s u e) -> p s u e", u=2, e=2)
-                    for up in range(2):
-                        for a in range(4):
-                            gl, u = a // 2, a % 2
-                            nc.tensor.matmul(
-                                z_view[:, :, up, :],
-                                lhsT=(h_neg if (gl * gp + u * up) % 2 else h_pos)[:],
-                                rhs=xt[:, 1024 * b + 256 * a : 1024 * b + 256 * (a + 1)].rearrange("p (s e) -> p s e", e=2),
-                                start=(a == 0),
-                                stop=(a == 3),
-                            )
-                    pairs = zb[:].rearrange("p (m e) -> p m e", e=2)
-                    odd = keep.tile([P, 2, 2 * P], F32, name="odd%d_%d" % (b, gp))
-                    for e in range(2):
-                        nc.scalar.mul(out=odd[:, e], in_=pairs[:, :, 1], mul=(-INV if e else INV))
-                    nc.vector.scalar_tensor_tensor(
-                        out=grouped[:, gp].rearrange("p s (u e) -> p (s u) e", e=2),
-                        in0=pairs[:, :, 0].unsqueeze(2).to_broadcast([P, 2 * P, 2]),
-                        scalar=INV,
-                        in1=odd[:].rearrange("p e m -> p m e"),
-                        op0=ALU.mult,
-                        op1=ALU.add,
-                    )
+                nc.tensor.matmul(zb[:], lhsT=h_pos[:], rhs=xt[:, 1024 * b : 1024 * b + 512], start=True, stop=False)
+                nc.tensor.matmul(
+                    zb[:],
+                    lhsT=(h_pos if gp == 0 else h_neg)[:],
+                    rhs=xt[:, 1024 * b + 512 : 1024 * (b + 1)],
+                    start=False,
+                    stop=True,
+                )
+                pairs = zb[:].rearrange("p (m e) -> p m e", e=2)
+                odd = keep.tile([P, 256], F32, name="odd%d_%d" % (b, gp))
+                nc.scalar.mul(out=odd[:], in_=pairs[:, :, 1], mul=INV)
+                nc.vector.scalar_tensor_tensor(
+                    out=stage_a[:, gp, 0, :], in0=pairs[:, :, 0], scalar=INV, in1=odd[:], op0=ALU.mult, op1=ALU.add
+                )
+                nc.vector.scalar_tensor_tensor(
+                    out=stage_a[:, gp, 1, :], in0=pairs[:, :, 0], scalar=INV, in1=odd[:], op0=ALU.mult, op1=ALU.subtract
+                )
+            yb = keep.tile([P, 2, 4, P], BF16, name="yb%d" % b)
+            nc.vector.tensor_tensor(
+                out=yb[:, :, 0:2, :], in0=stage_a[:, :, :, 0:P], in1=stage_a[:, :, :, P : 2 * P], op=ALU.add
+            )
+            nc.vector.tensor_tensor(
+                out=yb[:, :, 2:4, :], in0=stage_a[:, :, :, 0:P], in1=stage_a[:, :, :, P : 2 * P], op=ALU.subtract
+            )
+            grouped = keep.tile([P, 2, P, 4], BF16, name="grouped%d" % b, align_bytes=64)
+            nc.scalar.copy(out=grouped[:], in_=yb[:].rearrange("p g t s -> p g s t"))
             nc.vector.quantize_mx(
                 out=y_codes[:, 256 * b : 256 * (b + 1)].bitcast(FP8X4),
                 scales=y_planes[:, 256 * b : 256 * (b + 1)],

from contextlib import ExitStack

import concourse.mybir as mybir
from concourse.masks import make_identity

BF16 = mybir.dt.bfloat16
F32 = mybir.dt.float32
I32 = mybir.dt.int32
U8 = mybir.dt.uint8
U32 = mybir.dt.uint32
FP8X4 = mybir.dt.float8_e4m3fn_x4
ALU = mybir.AluOpType

P = 128
D = 4096
O = 4096
GROUPS = 8
NT = 512
BANKS = 8
INV = 1.0 / 32.0
MAIN = O - NT

FLOPS = 2 * 128 * 4096 * 4096 + 128 * 4096 * 10


def tile_hadlinear_w_kernel(tc, x_in, weight_words, weight_scales, out):
    nc = tc.nc
    xf = x_in.flatten_outer_dims()
    of = out.flatten_outer_dims()
    with ExitStack() as ctx:
        keep = ctx.enter_context(tc.tile_pool(name="keep", bufs=1))
        psum = ctx.enter_context(tc.psum_pool(name="psum", bufs=1))

        planes = keep.tile([P, 2, O], U8, name="planes", align_bytes=64)
        nc.vector.memset(planes[:].bitcast(I32), 0)
        x_sb = keep.tile([P, D], BF16, name="x_sb", align_bytes=64)
        for half in range(2):
            cols = slice(2048 * half, 2048 * (half + 1))
            nc.sync.dma_start(out=x_sb[:, cols], in_=xf[:, cols])
        words = weight_words.rearrange("g p n t -> p g (n t)").bitcast(I32)
        w_main = []
        for g in range(GROUPS):
            cuts = [0, MAIN] if g < GROUPS - 1 else [0, MAIN // 2 // NT * NT, MAIN]
            where = {}
            for lo, hi in zip(cuts[:-1], cuts[1:]):
                wt = keep.tile([P, hi - lo], U32, name="w%d_%d" % (g, lo), align_bytes=64)
                nc.sync.dma_start(out=wt[:].bitcast(I32), in_=words[:, g, lo:hi])
                for j in range(lo // NT, hi // NT):
                    where[j] = (wt, NT * j - lo)
            w_main.append(where)
        for lo, hi in ((0, 4), (4, 7), (7, 8)):
            wt = keep.tile([P, hi - lo, NT], U32, name="w_last%d" % lo, align_bytes=64)
            nc.sync.dma_start(out=wt[:].bitcast(I32), in_=words[:, lo:hi, MAIN:O])
            flat = wt[:].rearrange("p g n -> p (g n)")
            for g in range(lo, hi):
                w_main[g][BANKS - 1] = (flat, NT * (g - lo))

        ident = keep.tile([P, P], F32, name="ident")
        make_identity(nc, ident[:])
        ii = keep.tile([P, P], I32, name="ii")
        jj = keep.tile([P, P], I32, name="jj")
        nc.gpsimd.iota(ii[:], pattern=[[0, P]], base=0, channel_multiplier=1)
        nc.gpsimd.iota(jj[:], pattern=[[1, P]], base=0, channel_multiplier=0)
        for h in range(2):
            for q in range(4):
                nc.gpsimd.dma_start(
                    out=planes[32 * q : 32 * q + 16, h, :].bitcast(F32),
                    in_=weight_scales[4 * h : 4 * h + 4, 4 * q : 4 * q + 4, :].bitcast(F32),
                )
        par = keep.tile([P, P], I32, name="par")
        sh = keep.tile([P, P], I32, name="sh")
        nc.vector.tensor_tensor(out=par[:], in0=ii[:], in1=jj[:], op=ALU.bitwise_and)
        for s in (4, 2, 1):
            nc.vector.tensor_single_scalar(out=sh[:], in_=par[:], scalar=s, op=ALU.logical_shift_right)
            nc.vector.tensor_tensor(out=par[:], in0=par[:], in1=sh[:], op=ALU.bitwise_xor)
        nc.vector.tensor_single_scalar(out=par[:], in_=par[:], scalar=1, op=ALU.bitwise_and)
        h_pos = keep.tile([P, P], BF16, name="h_pos")
        h_neg = keep.tile([P, P], BF16, name="h_neg")
        nc.vector.tensor_scalar(out=h_pos[:], in0=par[:], scalar1=-2.0, scalar2=1.0, op0=ALU.mult, op1=ALU.add)
        nc.vector.tensor_scalar(out=h_neg[:], in0=par[:], scalar1=2.0, scalar2=-1.0, op0=ALU.mult, op1=ALU.add)

        xw = x_sb[:].bitcast(F32)
        xt = keep.tile([P, D], BF16, name="xt")
        for b in range(4):
            tb = psum.tile([P, 4, P], F32, name="tb%d" % b, tag="bank%d" % b)
            for a in range(4):
                g, u = 2 * b + a // 2, a % 2
                nc.tensor.transpose(tb[:, a, :], xw[:, 256 * g + u : 256 * (g + 1) : 2], ident[:])
            dst = xt[:, 1024 * b : 1024 * (b + 1)].bitcast(F32)
            src = tb[:].rearrange("p a s -> p (a s)")
            if b % 2 == 0:
                nc.vector.tensor_copy(out=dst, in_=src)
            else:
                nc.scalar.copy(out=dst, in_=src)

        y_codes = keep.tile([P, GROUPS * P], U32, name="y_codes", align_bytes=64)
        y_planes = keep.tile([P, GROUPS * P], U8, name="y_planes", align_bytes=64)
        z_banks = [(4, 5), (6, 7), (0, 1), (2, 3)]
        for b in range(4):
            stage_a = keep.tile([P, 2, 2, 256], F32, name="stage_a%d" % b)
            for gp in range(2):
                zb = psum.tile([P, NT], F32, name="z%d_%d" % (b, gp), tag="bank%d" % z_banks[b][gp])
                nc.tensor.matmul(zb[:], lhsT=h_pos[:], rhs=xt[:, 1024 * b : 1024 * b + 512], start=True, stop=False)
                nc.tensor.matmul(
                    zb[:],
                    lhsT=(h_pos if gp == 0 else h_neg)[:],
                    rhs=xt[:, 1024 * b + 512 : 1024 * (b + 1)],
                    start=False,
                    stop=True,
                )
                pairs = zb[:].rearrange("p (m e) -> p m e", e=2)
                odd = keep.tile([P, 256], F32, name="odd%d_%d" % (b, gp))
                nc.scalar.mul(out=odd[:], in_=pairs[:, :, 1], mul=INV)
                nc.vector.scalar_tensor_tensor(
                    out=stage_a[:, gp, 0, :], in0=pairs[:, :, 0], scalar=INV, in1=odd[:], op0=ALU.mult, op1=ALU.add
                )
                nc.vector.scalar_tensor_tensor(
                    out=stage_a[:, gp, 1, :], in0=pairs[:, :, 0], scalar=INV, in1=odd[:], op0=ALU.mult, op1=ALU.subtract
                )
            yb = keep.tile([P, 2, 4, P], BF16, name="yb%d" % b)
            nc.vector.tensor_tensor(
                out=yb[:, :, 0:2, :], in0=stage_a[:, :, :, 0:P], in1=stage_a[:, :, :, P : 2 * P], op=ALU.add
            )
            nc.vector.tensor_tensor(
                out=yb[:, :, 2:4, :], in0=stage_a[:, :, :, 0:P], in1=stage_a[:, :, :, P : 2 * P], op=ALU.subtract
            )
            grouped = keep.tile([P, 2, P, 4], BF16, name="grouped%d" % b, align_bytes=64)
            nc.scalar.copy(out=grouped[:], in_=yb[:].rearrange("p g t s -> p g s t"))
            nc.vector.quantize_mx(
                out=y_codes[:, 256 * b : 256 * (b + 1)].bitcast(FP8X4),
                scales=y_planes[:, 256 * b : 256 * (b + 1)],
                in_=grouped[:].rearrange("p g s t -> p (g s t)"),
            )

        acc = []
        for j in range(BANKS):
            acc.append(psum.tile([P, NT], F32, name="acc%d" % j, tag="bank%d" % ((j + 4) % BANKS)))
        passes = []
        for banks in ((0, 1, 2, 3), (4, 5, 6)):
            passes += [(g, j) for g in range(2) for j in banks]
        passes += [(g, j) for g in range(2, GROUPS) for j in range(BANKS - 1)]
        passes += [(g, BANKS - 1) for g in range(GROUPS)]
        for g, j in passes:
            k = 4 * (g % 4)
            h = g // 4
            wt, c = w_main[g][j]
            nc.tensor.matmul_mx(
                out=acc[j][:],
                lhsT=y_codes[:, P * g : P * (g + 1)].bitcast(FP8X4),
                lhsT_scale=y_planes[:, P * g : P * (g + 1)],
                rhs=wt[:, c : c + NT].bitcast(FP8X4),
                rhs_scale=planes[k:P, h, NT * j : NT * (j + 1)],
                start=(g == 0),
                stop=(g == GROUPS - 1),
            )
        for first, last in ((0, 1), (2, 3), (4, 5), (6, 6), (7, 7)):
            res = keep.tile([P, NT * (last - first + 1)], F32, name="res%d" % first)
            for j in range(first, last + 1):
                dst = res[:, NT * (j - first) : NT * (j - first + 1)]
                if j % 2 == 0:
                    nc.vector.tensor_copy(out=dst, in_=acc[j][:])
                else:
                    nc.scalar.copy(out=dst, in_=acc[j][:])
            nc.sync.dma_start(out=of[:, NT * first : NT * (last + 1)], in_=res[:])
